import numpy as np
import ml_dtypes


def mxq(x, axis, fmt="e4m3"):
    dtype, down = {"e4m3": (ml_dtypes.float8_e4m3fn, 7), "e5m2": (ml_dtypes.float8_e5m2, 14)}[fmt]
    v = np.moveaxis(np.asarray(x, np.float32).astype(ml_dtypes.bfloat16).astype(np.float64), axis, -1)
    blocks = v.reshape(v.shape[:-1] + (-1, 32))
    amax = np.abs(blocks).max(-1, keepdims=True)
    byte = np.maximum(np.where(amax > 0, np.frexp(amax)[1] - 1 + 127, 0) - down, 1)
    scale = np.exp2(byte - 127.0)
    codes = (blocks / scale).astype(np.float32).astype(dtype).astype(np.float64)
    return np.moveaxis((codes * scale).reshape(v.shape), -1, axis)


WIDE = False


def mx_kscale(k):
    if not WIDE:
        return np.ones(k)
    levels = np.array([10, -10, 5, -5, 0])
    a = np.random.permutation(np.resize(levels, k // 512 * 4)).reshape(k // 512, 4)
    idx = np.arange(k)
    return np.exp2(a[idx // 512, idx % 128 // 32])


BF16 = ml_dtypes.bfloat16


def bf(x):
    return np.asarray(x, np.float32).astype(BF16)


def f64(x):
    return np.asarray(x).astype(np.float64)


E2M1 = np.array([0.0, 0.5, 1.0, 1.5, 2.0, 3.0, 4.0, 6.0, -0.0, -0.5, -1.0, -1.5, -2.0, -3.0, -4.0, -6.0])


def pack_weight(w, fmt):
    k, n = w.shape
    w = f64(bf(w)).reshape(k // 32, 32, n)
    amax = np.abs(w).max(1)
    if fmt == "e4m3":
        byte = np.frexp(amax)[1] - 1 + 127 - 7
    else:
        mant, ex = np.frexp(amax / 6.0)
        byte = np.where(mant > 0.5, ex, ex - 1) + 127
    byte = np.clip(np.where(amax > 0, byte, 1), 1, 254)
    scaled = (w * np.exp2(127.0 - byte)[:, None, :]).reshape(k, n).astype(np.float32)
    by_word = np.ascontiguousarray(scaled.reshape(k // 512, 128, 4, n).transpose(0, 1, 3, 2))
    if fmt == "e4m3":
        words = by_word.astype(ml_dtypes.float8_e4m3fn).view(np.uint8)
    else:
        c = by_word.astype(ml_dtypes.float4_e2m1fn).view(np.uint8) & 0xF
        words = c[..., 0::2] | (c[..., 1::2] << 4)
    return np.ascontiguousarray(words), np.ascontiguousarray(byte.astype(np.uint8).reshape(k // 512, 16, n))


def unpack_weight(words, scales, fmt):
    g, p, n, _ = words.shape
    if fmt == "e4m3":
        vals = np.ascontiguousarray(words).view(ml_dtypes.float8_e4m3fn).astype(np.float64)
    else:
        nib = np.empty((g, p, n, 4), np.uint8)
        nib[..., 0::2] = words & 0xF
        nib[..., 1::2] = words >> 4
        vals = E2M1[nib]
    vals = vals * np.repeat(np.exp2(scales.astype(np.float64) - 127.0), 8, axis=1)[..., None]
    return vals.transpose(0, 1, 3, 2).reshape(g * 512, n)


B, R, C, H, DH = 16, 8, 1536, 12, 128
T = R * R
E = H * DH
EPS = 2.0 ** -23
FMT = "e4m3"


def rmsnorm(v):
    return v * (1.0 / np.sqrt(np.mean(np.square(v), axis=-1, keepdims=True) + EPS))


def setup_inputs():
    s = mx_kscale(C)
    x = bf(np.random.standard_normal((B, T, C)) * s)
    Wq_words, Wq_scales = pack_weight(np.random.standard_normal((C, E)) / np.sqrt(C) / s[:, None], FMT)
    Wk_words, Wk_scales = pack_weight(np.random.standard_normal((C, E)) / np.sqrt(C) / s[:, None], FMT)
    return {"x": x,
            "Wq_words": Wq_words, "Wq_scales": Wq_scales,
            "Wk_words": Wk_words, "Wk_scales": Wk_scales}


def reference(x, Wq_words, Wq_scales, Wk_words, Wk_scales):
    xq = mxq(f64(x), 2, "e4m3")

    def proj(words, scales):
        return (xq @ unpack_weight(words, scales, FMT)).reshape(B, T, H, DH).transpose(0, 2, 1, 3)

    return rmsnorm(proj(Wq_words, Wq_scales)), rmsnorm(proj(Wk_words, Wk_scales))

@@ -1,0 +1,196 @@
+from contextlib import ExitStack
+
+import concourse.masks as masks
+import concourse.mybir as mybir
+
+F32 = mybir.dt.float32
+BF16 = mybir.dt.bfloat16
+I32 = mybir.dt.int32
+U32 = mybir.dt.uint32
+U8 = mybir.dt.uint8
+FP8X4 = mybir.dt.float8_e4m3fn_x4
+ACT = mybir.ActivationFunctionType
+ALU = mybir.AluOpType
+
+P = 128
+PACK = 4
+K_PASS = P * PACK
+WORDS_PER_PASS = K_PASS // 2
+
+BOARDS, SQUARES, C = 16, 64, 1536
+HEADS, DH = 12, 128
+TOKENS = BOARDS * SQUARES
+TOKEN_TILES = TOKENS // P
+PAIRS = TOKEN_TILES // 2
+PASSES = C // K_PASS
+N_TILE = 512
+HEADS_PER_BANK = N_TILE // DH
+CHUNKS = HEADS * DH // N_TILE
+STORE_TILES = 4
+PAIRS_AHEAD = 2
+EPS = 2.0 ** -23
+
+FLOPS = 2 * TOKENS * C * 2 * HEADS * DH
+
+
+def tile_pieceroutedattention_pa_kernel(
+    tc, x, Wq_words, Wq_scales, Wk_words, Wk_scales, out_0, out_1
+):
+    nc = tc.nc
+    weight_words = (Wq_words, Wk_words)
+    weight_scales = (Wq_scales, Wk_scales)
+
+    x_tiles_dram = x.rearrange("b (s j) c -> (b s) j c", j=TOKEN_TILES)
+    out_heads_dram = [
+        out.rearrange("b h (s j) d -> h b s (j d)", j=TOKEN_TILES) for out in (out_0, out_1)
+    ]
+
+    with ExitStack() as ctx:
+        keep = ctx.enter_context(tc.tile_pool(name="keep", bufs=1))
+        group_pool = ctx.enter_context(tc.tile_pool(name="group", bufs=4))
+        stat_pool = ctx.enter_context(tc.tile_pool(name="stat", bufs=6))
+        square_pool = ctx.enter_context(tc.tile_pool(name="square", bufs=2))
+        stage_pool = ctx.enter_context(tc.tile_pool(name="stage", bufs=5))
+        psum = ctx.enter_context(tc.psum_pool(name="psum", bufs=8))
+
+        w_planes = [
+            keep.tile([P, HEADS * DH], U8, name="w_planes%d" % w, align_bytes=64) for w in range(2)
+        ]
+        for w in range(2):
+            nc.vector.memset(w_planes[w][:].bitcast(I32), 0)
+        eps = keep.tile([P, 1], F32, name="eps")
+        nc.vector.memset(eps[:], EPS)
+        ident = keep.tile([P, P], F32, name="ident")
+        masks.make_identity(nc, ident[:])
+        table_warm = keep.tile([P, 1], F32, name="table_warm")
+        nc.scalar.activation(out=table_warm[:], in_=eps[:], func=ACT.Abs_reciprocal_sqrt)
+
+        x_sb = [keep.tile([P, C], BF16, name="x%d" % j) for j in range(TOKEN_TILES)]
+        w_sb = [
+            [
+                keep.tile([P, PASSES, N_TILE * PACK], U8, name="w%d_%d" % (w, n), align_bytes=64)
+                for n in range(CHUNKS)
+            ]
+            for w in range(2)
+        ]
+
+        def load_x(j):
+            nc.sync.dma_start(out=x_sb[j][:], in_=x_tiles_dram[:, j, :])
+
+        def load_scales(w):
+            for quadrant in range(4):
+                nc.sync.dma_start(
+                    out=w_planes[w][32 * quadrant : 32 * quadrant + 4 * PASSES, :].bitcast(I32),
+                    in_=weight_scales[w][:, 4 * quadrant : 4 * quadrant + 4, :].bitcast(I32),
+                )
+
+        def load_words(w, n):
+            words = weight_words[w].rearrange("g p n t -> p g (n t)")
+            nc.sync.dma_start(
+                out=w_sb[w][n][:].bitcast(I32),
+                in_=words[:, :, N_TILE * PACK * n : N_TILE * PACK * (n + 1)].bitcast(I32),
+            )
+
+        load_x(0)
+        load_x(1)
+        load_scales(0)
+        load_scales(1)
+        load_words(0, 0)
+        for j in range(2, TOKEN_TILES):
+            load_x(j)
+        for w in range(2):
+            for n in range(CHUNKS):
+                if (w, n) != (0, 0):
+                    load_words(w, n)
+
+        x_codes = [
+            keep.tile([P, PASSES, 2 * P], U32, name="x_codes%d" % i, align_bytes=64)
+            for i in range(PAIRS)
+        ]
+        x_planes = [
+            keep.tile([P, PASSES, 2 * P], U8, name="x_planes%d" % i, align_bytes=64)
+            for i in range(PAIRS)
+        ]
+
+        def quantise_pair(pair):
+            for g in range(PASSES):
+                xt = psum.tile([P, 2, 2, P], F32, tag="bank")
+                for half in range(2):
+                    x_words = x_sb[2 * pair + half][:].bitcast(F32)
+                    for u in range(2):
+                        first = WORDS_PER_PASS * g + u
+                        nc.tensor.transpose(
+                            xt[:, half, u, :],
+                            x_words[:, first : WORDS_PER_PASS * (g + 1) : 2],
+                            ident[:],
+                        )
+                grouped = group_pool.tile([P, 2 * P * PACK], BF16, align_bytes=64)
+                grouped_words = grouped[:].bitcast(F32).rearrange(
+                    "p (half r u) -> p half r u", half=2, u=2
+                )
+                xt_by_token = xt[:].rearrange("p half u r -> p half r u")
+                if (pair * PASSES + g) % 2 == 0:
+                    nc.scalar.copy(out=grouped_words, in_=xt_by_token)
+                else:
+                    nc.vector.tensor_copy(out=grouped_words, in_=xt_by_token)
+                nc.vector.quantize_mx(
+                    out=x_codes[pair][:, g, :].bitcast(FP8X4),
+                    scales=x_planes[pair][:, g, :],
+                    in_=grouped[:],
+                )
+
+        def project(w, n, j, stage):
+            tokens = slice(P * (j % 2), P * (j % 2 + 1))
+            columns = slice(N_TILE * n, N_TILE * (n + 1))
+            acc = psum.tile([P, N_TILE], F32, tag="bank")
+            for g in range(PASSES):
+                nc.tensor.matmul_mx(
+                    out=acc[:],
+                    lhsT=x_codes[j // 2][:, g, tokens].bitcast(FP8X4),
+                    lhsT_scale=x_planes[j // 2][:, g, tokens],
+                    rhs=w_sb[w][n][:, g, :].bitcast(FP8X4),
+                    rhs_scale=w_planes[w][4 * g : P, columns],
+                    start=(g == 0),
+                    stop=(g == PASSES - 1),
+                )
+            squares = square_pool.tile([P, N_TILE], F32)
+            sum_sq = stat_pool.tile([P, HEADS_PER_BANK], F32)
+            for h in range(HEADS_PER_BANK):
+                head = slice(DH * h, DH * (h + 1))
+                nc.scalar.activation(
+                    out=squares[:, head],
+                    in_=acc[:, head],
+                    func=ACT.Square,
+                    accum_out=sum_sq[:, h : h + 1],
+                )
+            rstd = stat_pool.tile([P, HEADS_PER_BANK], F32)
+            nc.scalar.activation(
+                out=rstd[:], in_=sum_sq[:], func=ACT.Abs_reciprocal_sqrt, bias=eps[:], scale=1.0 / DH
+            )
+            nc.vector.tensor_tensor(
+                out=stage[:, :, j % STORE_TILES, :],
+                in0=acc[:].rearrange("p (h d) -> p h d", d=DH),
+                in1=rstd[:].unsqueeze(2).to_broadcast([P, HEADS_PER_BANK, DH]),
+                op=ALU.mult,
+            )
+
+        def store(w, n, first_tile, stage):
+            run = slice(DH * first_tile, DH * (first_tile + STORE_TILES))
+            for h in range(HEADS_PER_BANK):
+                nc.sync.dma_start(
+                    out=out_heads_dram[w][HEADS_PER_BANK * n + h, :, :, run],
+                    in_=stage[:, h, :, :].rearrange("p j d -> p (j d)"),
+                )
+
+        for pair in range(PAIRS_AHEAD):
+            quantise_pair(pair)
+        for w in range(2):
+            for n in range(CHUNKS):
+                for first_tile in range(0, TOKEN_TILES, STORE_TILES):
+                    stage = stage_pool.tile([P, HEADS_PER_BANK, STORE_TILES, DH], F32)
+                    for j in range(first_tile, first_tile + STORE_TILES):
+                        project(w, n, j, stage)
+                        next_pair = j // 2 + PAIRS_AHEAD
+                        if (w, n) == (0, 0) and j % 2 == 1 and next_pair < PAIRS:
+                            quantise_pair(next_pair)
+                    store(w, n, first_tile, stage)

@@ -27,7 +27,6 @@ N_TILE = 512
 HEADS_PER_BANK = N_TILE // DH
 CHUNKS = HEADS * DH // N_TILE
 STORE_TILES = 4
-PAIRS_AHEAD = 2
 EPS = 2.0 ** -23
 
 FLOPS = 2 * TOKENS * C * 2 * HEADS * DH
@@ -52,6 +51,7 @@ def tile_pieceroutedattention_pa_kernel(
         square_pool = ctx.enter_context(tc.tile_pool(name="square", bufs=2))
         stage_pool = ctx.enter_context(tc.tile_pool(name="stage", bufs=5))
         psum = ctx.enter_context(tc.psum_pool(name="psum", bufs=8))
+        ctx.enter_context(tc.manual_schedule())
 
         w_planes = [
             keep.tile([P, HEADS * DH], U8, name="w_planes%d" % w, align_bytes=64) for w in range(2)
@@ -95,13 +95,11 @@ def tile_pieceroutedattention_pa_kernel(
         load_x(1)
         load_scales(0)
         load_scales(1)
-        load_words(0, 0)
         for j in range(2, TOKEN_TILES):
             load_x(j)
         for w in range(2):
             for n in range(CHUNKS):
-                if (w, n) != (0, 0):
-                    load_words(w, n)
+                load_words(w, n)
 
         x_codes = [
             keep.tile([P, PASSES, 2 * P], U32, name="x_codes%d" % i, align_bytes=64)
@@ -112,34 +110,45 @@ def tile_pieceroutedattention_pa_kernel(
             for i in range(PAIRS)
         ]
 
-        def quantise_pair(pair):
-            for g in range(PASSES):
-                xt = psum.tile([P, 2, 2, P], F32, tag="bank")
-                for half in range(2):
-                    x_words = x_sb[2 * pair + half][:].bitcast(F32)
-                    for u in range(2):
-                        first = WORDS_PER_PASS * g + u
-                        nc.tensor.transpose(
-                            xt[:, half, u, :],
-                            x_words[:, first : WORDS_PER_PASS * (g + 1) : 2],
-                            ident[:],
-                        )
-                grouped = group_pool.tile([P, 2 * P * PACK], BF16, align_bytes=64)
-                grouped_words = grouped[:].bitcast(F32).rearrange(
-                    "p (half r u) -> p half r u", half=2, u=2
-                )
-                xt_by_token = xt[:].rearrange("p half u r -> p half r u")
-                if (pair * PASSES + g) % 2 == 0:
-                    nc.scalar.copy(out=grouped_words, in_=xt_by_token)
-                else:
-                    nc.vector.tensor_copy(out=grouped_words, in_=xt_by_token)
-                nc.vector.quantize_mx(
-                    out=x_codes[pair][:, g, :].bitcast(FP8X4),
-                    scales=x_planes[pair][:, g, :],
-                    in_=grouped[:],
-                )
+        def transpose_unit(pair, g):
+            xt = psum.tile([P, 2, 2, P], F32, tag="bank")
+            for half in range(2):
+                x_words = x_sb[2 * pair + half][:].bitcast(F32)
+                for u in range(2):
+                    first = WORDS_PER_PASS * g + u
+                    nc.tensor.transpose(
+                        xt[:, half, u, :],
+                        x_words[:, first : WORDS_PER_PASS * (g + 1) : 2],
+                        ident[:],
+                    )
+            grouped = group_pool.tile([P, 2 * P * PACK], BF16, align_bytes=64)
+            grouped_words = grouped[:].bitcast(F32).rearrange(
+                "p (half r u) -> p half r u", half=2, u=2
+            )
+            xt_by_token = xt[:].rearrange("p half u r -> p half r u")
+            if g == 0:
+                nc.vector.tensor_copy(out=grouped_words, in_=xt_by_token)
+            else:
+                nc.scalar.copy(out=grouped_words, in_=xt_by_token)
+            return grouped
 
-        def project(w, n, j, stage):
+        def quantise_unit(pair, g, grouped):
+            nc.vector.quantize_mx(
+                out=x_codes[pair][:, g, :].bitcast(FP8X4),
+                scales=x_planes[pair][:, g, :],
+                in_=grouped[:],
+            )
+
+        copied = None
+        for pair in range(PAIRS):
+            for g in range(PASSES):
+                grouped = transpose_unit(pair, g)
+                if copied is not None:
+                    quantise_unit(*copied)
+                copied = (pair, g, grouped)
+        quantise_unit(*copied)
+
+        def project(w, n, j):
             tokens = slice(P * (j % 2), P * (j % 2 + 1))
             columns = slice(N_TILE * n, N_TILE * (n + 1))
             acc = psum.tile([P, N_TILE], F32, tag="bank")
@@ -163,12 +172,15 @@ def tile_pieceroutedattention_pa_kernel(
                     func=ACT.Square,
                     accum_out=sum_sq[:, h : h + 1],
                 )
+            return acc, sum_sq
+
+        def normalise(acc, sum_sq, stage_columns):
             rstd = stat_pool.tile([P, HEADS_PER_BANK], F32)
             nc.scalar.activation(
                 out=rstd[:], in_=sum_sq[:], func=ACT.Abs_reciprocal_sqrt, bias=eps[:], scale=1.0 / DH
             )
             nc.vector.tensor_tensor(
-                out=stage[:, :, j % STORE_TILES, :],
+                out=stage_columns,
                 in0=acc[:].rearrange("p (h d) -> p h d", d=DH),
                 in1=rstd[:].unsqueeze(2).to_broadcast([P, HEADS_PER_BANK, DH]),
                 op=ALU.mult,
@@ -182,15 +194,19 @@ def tile_pieceroutedattention_pa_kernel(
                     in_=stage[:, h, :, :].rearrange("p j d -> p (j d)"),
                 )
 
-        for pair in range(PAIRS_AHEAD):
-            quantise_pair(pair)
+        def finish(w, n, j, acc, sum_sq, stage):
+            normalise(acc, sum_sq, stage[:, :, j % STORE_TILES, :])
+            if j % STORE_TILES == STORE_TILES - 1:
+                store(w, n, j - (STORE_TILES - 1), stage)
+
+        squared = None
         for w in range(2):
             for n in range(CHUNKS):
-                for first_tile in range(0, TOKEN_TILES, STORE_TILES):
-                    stage = stage_pool.tile([P, HEADS_PER_BANK, STORE_TILES, DH], F32)
-                    for j in range(first_tile, first_tile + STORE_TILES):
-                        project(w, n, j, stage)
-                        next_pair = j // 2 + PAIRS_AHEAD
-                        if (w, n) == (0, 0) and j % 2 == 1 and next_pair < PAIRS:
-                            quantise_pair(next_pair)
-                    store(w, n, first_tile, stage)
+                for j in range(TOKEN_TILES):
+                    if j % STORE_TILES == 0:
+                        stage = stage_pool.tile([P, HEADS_PER_BANK, STORE_TILES, DH], F32)
+                    acc, sum_sq = project(w, n, j)
+                    if squared is not None:
+                        finish(*squared)
+                    squared = (w, n, j, acc, sum_sq, stage)
+        finish(*squared)

@@ -91,15 +91,13 @@ def tile_pieceroutedattention_pa_kernel(
                 in_=words[:, :, N_TILE * PACK * n : N_TILE * PACK * (n + 1)].bitcast(I32),
             )
 
-        load_x(0)
-        load_x(1)
-        load_scales(0)
-        load_scales(1)
-        for j in range(2, TOKEN_TILES):
+        for j in range(TOKEN_TILES):
             load_x(j)
         for w in range(2):
             for n in range(CHUNKS):
                 load_words(w, n)
+                if n == 0:
+                    load_scales(w)
 
         x_codes = [
             keep.tile([P, PASSES, 2 * P], U32, name="x_codes%d" % i, align_bytes=64)

@@ -26,7 +26,9 @@ PASSES = C // K_PASS
 N_TILE = 512
 HEADS_PER_BANK = N_TILE // DH
 CHUNKS = HEADS * DH // N_TILE
-STORE_TILES = 4
+HEADS_PER_SWEEP = 2
+N_SWEEP = HEADS_PER_SWEEP * DH
+SWEEPS = HEADS // HEADS_PER_SWEEP
 EPS = 2.0 ** -23
 
 FLOPS = 2 * TOKENS * C * 2 * HEADS * DH
@@ -49,7 +51,7 @@ def tile_pieceroutedattention_pa_kernel(
         group_pool = ctx.enter_context(tc.tile_pool(name="group", bufs=4))
         stat_pool = ctx.enter_context(tc.tile_pool(name="stat", bufs=6))
         square_pool = ctx.enter_context(tc.tile_pool(name="square", bufs=2))
-        stage_pool = ctx.enter_context(tc.tile_pool(name="stage", bufs=5))
+        stage_pool = ctx.enter_context(tc.tile_pool(name="stage", bufs=4))
         psum = ctx.enter_context(tc.psum_pool(name="psum", bufs=8))
         ctx.enter_context(tc.manual_schedule())
 
@@ -84,20 +86,25 @@ def tile_pieceroutedattention_pa_kernel(
                     in_=weight_scales[w][:, 4 * quadrant : 4 * quadrant + 4, :].bitcast(I32),
                 )
 
-        def load_words(w, n):
+        def load_words(w, n, first_byte, n_bytes):
             words = weight_words[w].rearrange("g p n t -> p g (n t)")
+            start = N_TILE * PACK * n + first_byte
             nc.sync.dma_start(
-                out=w_sb[w][n][:].bitcast(I32),
-                in_=words[:, :, N_TILE * PACK * n : N_TILE * PACK * (n + 1)].bitcast(I32),
+                out=w_sb[w][n][:, :, first_byte : first_byte + n_bytes].bitcast(I32),
+                in_=words[:, :, start : start + n_bytes].bitcast(I32),
             )
 
         for j in range(TOKEN_TILES):
             load_x(j)
-        for w in range(2):
-            for n in range(CHUNKS):
-                load_words(w, n)
-                if n == 0:
-                    load_scales(w)
+        load_scales(0)
+        load_words(0, 0, 0, N_SWEEP * PACK)
+        load_words(0, 0, N_SWEEP * PACK, N_SWEEP * PACK)
+        load_words(0, 1, 0, N_TILE * PACK)
+        load_words(0, 2, 0, N_TILE * PACK)
+        load_words(1, 0, 0, N_TILE * PACK)
+        load_scales(1)
+        load_words(1, 1, 0, N_TILE * PACK)
+        load_words(1, 2, 0, N_TILE * PACK)
 
         x_codes = [
             keep.tile([P, PASSES, 2 * P], U32, name="x_codes%d" % i, align_bytes=64)
@@ -108,17 +115,17 @@ def tile_pieceroutedattention_pa_kernel(
             for i in range(PAIRS)
         ]
 
-        def transpose_unit(pair, g):
-            xt = psum.tile([P, 2, 2, P], F32, tag="bank")
-            for half in range(2):
-                x_words = x_sb[2 * pair + half][:].bitcast(F32)
-                for u in range(2):
-                    first = WORDS_PER_PASS * g + u
-                    nc.tensor.transpose(
-                        xt[:, half, u, :],
-                        x_words[:, first : WORDS_PER_PASS * (g + 1) : 2],
-                        ident[:],
-                    )
+        def transpose_words(pair, half, g, xt):
+            x_words = x_sb[2 * pair + half][:].bitcast(F32)
+            for u in range(2):
+                first = WORDS_PER_PASS * g + u
+                nc.tensor.transpose(
+                    xt[:, half, u, :],
+                    x_words[:, first : WORDS_PER_PASS * (g + 1) : 2],
+                    ident[:],
+                )
+
+        def regroup(g, xt):
             grouped = group_pool.tile([P, 2 * P * PACK], BF16, align_bytes=64)
             grouped_words = grouped[:].bitcast(F32).rearrange(
                 "p (half r u) -> p half r u", half=2, u=2
@@ -139,72 +146,125 @@ def tile_pieceroutedattention_pa_kernel(
 
         copied = None
         for pair in range(PAIRS):
+            banks = []
             for g in range(PASSES):
-                grouped = transpose_unit(pair, g)
+                xt = psum.tile([P, 2, 2, P], F32, tag="bank")
+                banks.append(xt)
+                transpose_words(pair, 0, g, xt)
+            for g in range(PASSES):
+                transpose_words(pair, 1, g, banks[g])
+                grouped = regroup(g, banks[g])
                 if copied is not None:
                     quantise_unit(*copied)
                 copied = (pair, g, grouped)
         quantise_unit(*copied)
 
-        def project(w, n, j):
-            tokens = slice(P * (j % 2), P * (j % 2 + 1))
-            columns = slice(N_TILE * n, N_TILE * (n + 1))
+        def project(w, s, tiles, first_head, n_heads):
+            n, side = divmod(s, N_TILE // N_SWEEP)
+            width = DH * n_heads
+            first_word = N_SWEEP * side + DH * first_head
+            word_bytes = slice(PACK * first_word, PACK * (first_word + width))
+            columns = slice(N_SWEEP * s + DH * first_head, N_SWEEP * s + DH * first_head + width)
             acc = psum.tile([P, N_TILE], F32, tag="bank")
-            for g in range(PASSES):
-                nc.tensor.matmul_mx(
-                    out=acc[:],
-                    lhsT=x_codes[j // 2][:, g, tokens].bitcast(FP8X4),
-                    lhsT_scale=x_planes[j // 2][:, g, tokens],
-                    rhs=w_sb[w][n][:, g, :].bitcast(FP8X4),
-                    rhs_scale=w_planes[w][4 * g : P, columns],
-                    start=(g == 0),
-                    stop=(g == PASSES - 1),
-                )
-            squares = square_pool.tile([P, N_TILE], F32)
-            sum_sq = stat_pool.tile([P, HEADS_PER_BANK], F32)
-            for h in range(HEADS_PER_BANK):
-                head = slice(DH * h, DH * (h + 1))
-                nc.scalar.activation(
-                    out=squares[:, head],
-                    in_=acc[:, head],
-                    func=ACT.Square,
-                    accum_out=sum_sq[:, h : h + 1],
-                )
-            return acc, sum_sq
+            for i, j in enumerate(tiles):
+                tokens = slice(P * (j % 2), P * (j % 2 + 1))
+                for g in range(PASSES):
+                    nc.tensor.matmul_mx(
+                        out=acc[:, width * i : width * (i + 1)],
+                        lhsT=x_codes[j // 2][:, g, tokens].bitcast(FP8X4),
+                        lhsT_scale=x_planes[j // 2][:, g, tokens],
+                        rhs=w_sb[w][n][:, g, word_bytes].bitcast(FP8X4),
+                        rhs_scale=w_planes[w][4 * g : P, columns],
+                        start=(g == 0),
+                        stop=(g == PASSES - 1),
+                    )
+            return acc
 
-        def normalise(acc, sum_sq, stage_columns):
-            rstd = stat_pool.tile([P, HEADS_PER_BANK], F32)
+        def sum_squares(acc, squares, sum_sq, first, count):
+            for q in range(first, first + count):
+                vector = slice(DH * q, DH * (q + 1))
+                nc.scalar.activation(
+                    out=squares[:, vector],
+                    in_=acc[:, vector],
+                    func=ACT.Square,
+                    accum_out=sum_sq[:, q : q + 1],
+                )
+
+        def normalise(acc, sum_sq, tiles, first_head, n_heads, stage):
+            count = len(tiles) * n_heads
+            rstd = stat_pool.tile([P, N_TILE // DH], F32)
             nc.scalar.activation(
-                out=rstd[:], in_=sum_sq[:], func=ACT.Abs_reciprocal_sqrt, bias=eps[:], scale=1.0 / DH
+                out=rstd[:, 0:count],
+                in_=sum_sq[:, 0:count],
+                func=ACT.Abs_reciprocal_sqrt,
+                bias=eps[:],
+                scale=1.0 / DH,
             )
             nc.vector.tensor_tensor(
-                out=stage_columns,
-                in0=acc[:].rearrange("p (h d) -> p h d", d=DH),
-                in1=rstd[:].unsqueeze(2).to_broadcast([P, HEADS_PER_BANK, DH]),
+                out=stage[
+                    :, first_head : first_head + n_heads, tiles[0] : tiles[0] + len(tiles), :
+                ].rearrange("p h j d -> p j h d"),
+                in0=acc[:, 0 : DH * count].rearrange("p (j h d) -> p j h d", h=n_heads, d=DH),
+                in1=rstd[:, 0:count]
+                .rearrange("p (j h) -> p j h", h=n_heads)
+                .unsqueeze(3)
+                .to_broadcast([P, len(tiles), n_heads, DH]),
                 op=ALU.mult,
             )
 
-        def store(w, n, first_tile, stage):
-            run = slice(DH * first_tile, DH * (first_tile + STORE_TILES))
-            for h in range(HEADS_PER_BANK):
-                nc.sync.dma_start(
-                    out=out_heads_dram[w][HEADS_PER_BANK * n + h, :, :, run],
-                    in_=stage[:, h, :, :].rearrange("p j d -> p (j d)"),
-                )
+        def store(w, s, head, first_tile, n_tiles, stage):
+            nc.sync.dma_start(
+                out=out_heads_dram[w][
+                    HEADS_PER_SWEEP * s + head, :, :, DH * first_tile : DH * (first_tile + n_tiles)
+                ],
+                in_=stage[:, head, first_tile : first_tile + n_tiles, :].rearrange(
+                    "p j d -> p (j d)"
+                ),
+            )
 
-        def finish(w, n, j, acc, sum_sq, stage):
-            normalise(acc, sum_sq, stage[:, :, j % STORE_TILES, :])
-            if j % STORE_TILES == STORE_TILES - 1:
-                store(w, n, j - (STORE_TILES - 1), stage)
+        def finish(w, s, tiles, first_head, n_heads, stores, acc, sum_sq, stage):
+            normalise(acc, sum_sq, tiles, first_head, n_heads, stage)
+            for head, first_tile, n_tiles in stores:
+                store(w, s, head, first_tile, n_tiles, stage)
+
+        sweep_pieces = [
+            ((0, 1), 0, 2, []),
+            ((2, 3), 0, 2, []),
+            ((4, 5), 0, 2, []),
+            ((6, 7), 0, 2, [(0, 0, 8), (1, 0, 8)]),
+        ]
+        before_last_pieces = [
+            ((0, 1), 0, 2, []),
+            ((2, 3), 0, 2, [(0, 0, 4), (1, 0, 4)]),
+            ((4, 5), 0, 2, []),
+            ((6, 7), 0, 2, [(0, 4, 4), (1, 4, 4)]),
+        ]
+        last_sweep_pieces = [
+            ((0, 1), 0, 2, [(0, 0, 2), (1, 0, 2)]),
+            ((2, 3), 0, 2, [(0, 2, 2), (1, 2, 2)]),
+            ((4, 5), 0, 2, [(0, 4, 2), (1, 4, 2)]),
+            ((6,), 0, 2, []),
+            ((7,), 0, 1, [(0, 6, 2)]),
+            ((7,), 1, 1, [(1, 6, 2)]),
+        ]
 
         squared = None
         for w in range(2):
-            for n in range(CHUNKS):
-                for j in range(TOKEN_TILES):
-                    if j % STORE_TILES == 0:
-                        stage = stage_pool.tile([P, HEADS_PER_BANK, STORE_TILES, DH], F32)
-                    acc, sum_sq = project(w, n, j)
+            for s in range(SWEEPS):
+                stage = stage_pool.tile([P, HEADS_PER_SWEEP, TOKEN_TILES, DH], F32)
+                last_sweep = w == 1 and s == SWEEPS - 1
+                before_last = w == 1 and s == SWEEPS - 2
+                for tiles, first_head, n_heads, stores in (
+                    last_sweep_pieces
+                    if last_sweep
+                    else (before_last_pieces if before_last else sweep_pieces)
+                ):
+                    acc = project(w, s, tiles, first_head, n_heads)
+                    squares = square_pool.tile([P, N_TILE], F32)
+                    sum_sq = stat_pool.tile([P, N_TILE // DH], F32)
+                    sum_squares(acc, squares, sum_sq, 0, 1)
                     if squared is not None:
                         finish(*squared)
-                    squared = (w, n, j, acc, sum_sq, stage)
+                    sum_squares(acc, squares, sum_sq, 1, len(tiles) * n_heads - 1)
+                    squared = (w, s, tiles, first_head, n_heads, stores, acc, sum_sq, stage)
         finish(*squared)

@@ -58,8 +58,7 @@ def tile_pieceroutedattention_pa_kernel(
         w_planes = [
             keep.tile([P, HEADS * DH], U8, name="w_planes%d" % w, align_bytes=64) for w in range(2)
         ]
-        for w in range(2):
-            nc.vector.memset(w_planes[w][:].bitcast(I32), 0)
+        nc.vector.memset(w_planes[0][:].bitcast(I32), 0)
         eps = keep.tile([P, 1], F32, name="eps")
         nc.vector.memset(eps[:], EPS)
         ident = keep.tile([P, P], F32, name="ident")
@@ -81,9 +80,9 @@ def tile_pieceroutedattention_pa_kernel(
 
         def load_scales(w):
             for quadrant in range(4):
-                nc.sync.dma_start(
-                    out=w_planes[w][32 * quadrant : 32 * quadrant + 4 * PASSES, :].bitcast(I32),
-                    in_=weight_scales[w][:, 4 * quadrant : 4 * quadrant + 4, :].bitcast(I32),
+                nc.gpsimd.dma_start(
+                    out=w_planes[w][32 * quadrant : 32 * quadrant + 4 * PASSES, :].bitcast(F32),
+                    in_=weight_scales[w][:, 4 * quadrant : 4 * quadrant + 4, :].bitcast(F32),
                 )
 
         def load_words(w, n, first_byte, n_bytes):
@@ -94,17 +93,15 @@ def tile_pieceroutedattention_pa_kernel(
                 in_=words[:, :, start : start + n_bytes].bitcast(I32),
             )
 
+        load_scales(0)
         for j in range(TOKEN_TILES):
             load_x(j)
-        load_scales(0)
         load_words(0, 0, 0, N_SWEEP * PACK)
         load_words(0, 0, N_SWEEP * PACK, N_SWEEP * PACK)
-        load_words(0, 1, 0, N_TILE * PACK)
-        load_words(0, 2, 0, N_TILE * PACK)
-        load_words(1, 0, 0, N_TILE * PACK)
-        load_scales(1)
-        load_words(1, 1, 0, N_TILE * PACK)
-        load_words(1, 2, 0, N_TILE * PACK)
+        for w in range(2):
+            for n in range(CHUNKS):
+                if w + n > 0:
+                    load_words(w, n, 0, N_TILE * PACK)
 
         x_codes = [
             keep.tile([P, PASSES, 2 * P], U32, name="x_codes%d" % i, align_bytes=64)
@@ -158,6 +155,9 @@ def tile_pieceroutedattention_pa_kernel(
                     quantise_unit(*copied)
                 copied = (pair, g, grouped)
         quantise_unit(*copied)
+
+        nc.vector.memset(w_planes[1][:].bitcast(I32), 0)
+        load_scales(1)
 
         def project(w, s, tiles, first_head, n_heads):
             n, side = divmod(s, N_TILE // N_SWEEP)

@@ -56,7 +56,7 @@ def tile_pieceroutedattention_pa_kernel(
         ctx.enter_context(tc.manual_schedule())
 
         w_planes = [
-            keep.tile([P, HEADS * DH], U8, name="w_planes%d" % w, align_bytes=64) for w in range(2)
+            keep.tile([P, HEADS * DH], U8, name="w_planes%d" % w, align_bytes=256) for w in range(2)
         ]
         nc.vector.memset(w_planes[0][:].bitcast(I32), 0)
         eps = keep.tile([P, 1], F32, name="eps")
@@ -69,7 +69,7 @@ def tile_pieceroutedattention_pa_kernel(
         x_sb = [keep.tile([P, C], BF16, name="x%d" % j) for j in range(TOKEN_TILES)]
         w_sb = [
             [
-                keep.tile([P, PASSES, N_TILE * PACK], U8, name="w%d_%d" % (w, n), align_bytes=64)
+                keep.tile([P, PASSES, N_TILE * PACK], U8, name="w%d_%d" % (w, n), align_bytes=256)
                 for n in range(CHUNKS)
             ]
             for w in range(2)
@@ -104,11 +104,11 @@ def tile_pieceroutedattention_pa_kernel(
                     load_words(w, n, 0, N_TILE * PACK)
 
         x_codes = [
-            keep.tile([P, PASSES, 2 * P], U32, name="x_codes%d" % i, align_bytes=64)
+            keep.tile([P, PASSES, 2 * P], U32, name="x_codes%d" % i, align_bytes=256)
             for i in range(PAIRS)
         ]
         x_planes = [
-            keep.tile([P, PASSES, 2 * P], U8, name="x_planes%d" % i, align_bytes=64)
+            keep.tile([P, PASSES, 2, 2 * P], U8, name="x_planes%d" % i, align_bytes=256)
             for i in range(PAIRS)
         ]
 
@@ -123,7 +123,7 @@ def tile_pieceroutedattention_pa_kernel(
                 )
 
         def regroup(g, xt):
-            grouped = group_pool.tile([P, 2 * P * PACK], BF16, align_bytes=64)
+            grouped = group_pool.tile([P, 2 * P * PACK], BF16, align_bytes=256)
             grouped_words = grouped[:].bitcast(F32).rearrange(
                 "p (half r u) -> p half r u", half=2, u=2
             )
@@ -135,11 +135,12 @@ def tile_pieceroutedattention_pa_kernel(
             return grouped
 
         def quantise_unit(pair, g, grouped):
-            nc.vector.quantize_mx(
-                out=x_codes[pair][:, g, :].bitcast(FP8X4),
-                scales=x_planes[pair][:, g, :],
-                in_=grouped[:],
-            )
+            for half in range(2):
+                nc.vector.quantize_mx(
+                    out=x_codes[pair][:, g, P * half : P * (half + 1)].bitcast(FP8X4),
+                    scales=x_planes[pair][:, g, half, 0:P],
+                    in_=grouped[:, P * PACK * half : P * PACK * (half + 1)],
+                )
 
         copied = None
         for pair in range(PAIRS):
@@ -172,7 +173,7 @@ def tile_pieceroutedattention_pa_kernel(
                     nc.tensor.matmul_mx(
                         out=acc[:, width * i : width * (i + 1)],
                         lhsT=x_codes[j // 2][:, g, tokens].bitcast(FP8X4),
-                        lhsT_scale=x_planes[j // 2][:, g, tokens],
+                        lhsT_scale=x_planes[j // 2][:, g, j % 2, 0:P],
                         rhs=w_sb[w][n][:, g, word_bytes].bitcast(FP8X4),
                         rhs_scale=w_planes[w][4 * g : P, columns],
                         start=(g == 0),

@@ -51,7 +51,8 @@ def tile_pieceroutedattention_pa_kernel(
         group_pool = ctx.enter_context(tc.tile_pool(name="group", bufs=4))
         stat_pool = ctx.enter_context(tc.tile_pool(name="stat", bufs=6))
         square_pool = ctx.enter_context(tc.tile_pool(name="square", bufs=2))
-        stage_pool = ctx.enter_context(tc.tile_pool(name="stage", bufs=4))
+        stage_pool = ctx.enter_context(tc.tile_pool(name="stage", bufs=3))
+        wide_stage_pool = ctx.enter_context(tc.tile_pool(name="wide_stage", bufs=3))
         psum = ctx.enter_context(tc.psum_pool(name="psum", bufs=8))
         ctx.enter_context(tc.manual_schedule())
 
@@ -160,12 +161,12 @@ def tile_pieceroutedattention_pa_kernel(
         nc.vector.memset(w_planes[1][:].bitcast(I32), 0)
         load_scales(1)
 
-        def project(w, s, tiles, first_head, n_heads):
-            n, side = divmod(s, N_TILE // N_SWEEP)
+        def project(w, base, tiles, first_head, n_heads):
+            n, head_in_chunk = divmod(base + first_head, HEADS_PER_BANK)
             width = DH * n_heads
-            first_word = N_SWEEP * side + DH * first_head
+            first_word = DH * head_in_chunk
             word_bytes = slice(PACK * first_word, PACK * (first_word + width))
-            columns = slice(N_SWEEP * s + DH * first_head, N_SWEEP * s + DH * first_head + width)
+            columns = slice(DH * (base + first_head), DH * (base + first_head) + width)
             acc = psum.tile([P, N_TILE], F32, tag="bank")
             for i, j in enumerate(tiles):
                 tokens = slice(P * (j % 2), P * (j % 2 + 1))
@@ -213,26 +214,35 @@ def tile_pieceroutedattention_pa_kernel(
                 op=ALU.mult,
             )
 
-        def store(w, s, head, first_tile, n_tiles, stage):
+        def store(w, base, head, first_tile, n_tiles, stage):
             nc.sync.dma_start(
                 out=out_heads_dram[w][
-                    HEADS_PER_SWEEP * s + head, :, :, DH * first_tile : DH * (first_tile + n_tiles)
+                    base + head, :, :, DH * first_tile : DH * (first_tile + n_tiles)
                 ],
                 in_=stage[:, head, first_tile : first_tile + n_tiles, :].rearrange(
                     "p j d -> p (j d)"
                 ),
             )
 
-        def finish(w, s, tiles, first_head, n_heads, stores, acc, sum_sq, stage):
+        def finish(w, base, tiles, first_head, n_heads, stores, acc, sum_sq, stage):
             normalise(acc, sum_sq, tiles, first_head, n_heads, stage)
             for head, first_tile, n_tiles in stores:
-                store(w, s, head, first_tile, n_tiles, stage)
+                store(w, base, head, first_tile, n_tiles, stage)
 
         sweep_pieces = [
             ((0, 1), 0, 2, []),
             ((2, 3), 0, 2, []),
             ((4, 5), 0, 2, []),
             ((6, 7), 0, 2, [(0, 0, 8), (1, 0, 8)]),
+        ]
+        wide_pieces = [
+            (
+                (j,),
+                0,
+                HEADS_PER_BANK,
+                [(h, j - 3, 4) for h in range(HEADS_PER_BANK)] if j % 4 == 3 else [],
+            )
+            for j in range(TOKEN_TILES)
         ]
         before_last_pieces = [
             ((0, 1), 0, 2, []),
@@ -249,23 +259,29 @@ def tile_pieceroutedattention_pa_kernel(
             ((7,), 1, 1, [(1, 6, 2)]),
         ]
 
+        sweeps = [
+            (0, 0, sweep_pieces),
+            (0, 2, sweep_pieces),
+            (0, 4, wide_pieces),
+            (0, 8, wide_pieces),
+            (1, 0, wide_pieces),
+            (1, 4, wide_pieces),
+            (1, 8, before_last_pieces),
+            (1, 10, last_sweep_pieces),
+        ]
         squared = None
-        for w in range(2):
-            for s in range(SWEEPS):
+        for w, base, pieces in sweeps:
+            if pieces[0][2] == HEADS_PER_BANK:
+                stage = wide_stage_pool.tile([P, HEADS_PER_BANK, TOKEN_TILES, DH], F32)
+            else:
                 stage = stage_pool.tile([P, HEADS_PER_SWEEP, TOKEN_TILES, DH], F32)
-                last_sweep = w == 1 and s == SWEEPS - 1
-                before_last = w == 1 and s == SWEEPS - 2
-                for tiles, first_head, n_heads, stores in (
-                    last_sweep_pieces
-                    if last_sweep
-                    else (before_last_pieces if before_last else sweep_pieces)
-                ):
-                    acc = project(w, s, tiles, first_head, n_heads)
-                    squares = square_pool.tile([P, N_TILE], F32)
-                    sum_sq = stat_pool.tile([P, N_TILE // DH], F32)
-                    sum_squares(acc, squares, sum_sq, 0, 1)
-                    if squared is not None:
-                        finish(*squared)
-                    sum_squares(acc, squares, sum_sq, 1, len(tiles) * n_heads - 1)
-                    squared = (w, s, tiles, first_head, n_heads, stores, acc, sum_sq, stage)
+            for tiles, first_head, n_heads, stores in pieces:
+                acc = project(w, base, tiles, first_head, n_heads)
+                squares = square_pool.tile([P, N_TILE], F32)
+                sum_sq = stat_pool.tile([P, N_TILE // DH], F32)
+                sum_squares(acc, squares, sum_sq, 0, 1)
+                if squared is not None:
+                    finish(*squared)
+                sum_squares(acc, squares, sum_sq, 1, len(tiles) * n_heads - 1)
+                squared = (w, base, tiles, first_head, n_heads, stores, acc, sum_sq, stage)
         finish(*squared)

@@ -67,7 +67,7 @@ def tile_pieceroutedattention_pa_kernel(
         table_warm = keep.tile([P, 1], F32, name="table_warm")
         nc.scalar.activation(out=table_warm[:], in_=eps[:], func=ACT.Abs_reciprocal_sqrt)
 
-        x_sb = [keep.tile([P, C], BF16, name="x%d" % j) for j in range(TOKEN_TILES)]
+        x_sb = [keep.tile([P, 2, C], BF16, name="x%d" % i) for i in range(PAIRS)]
         w_sb = [
             [
                 keep.tile([P, PASSES, N_TILE * PACK], U8, name="w%d_%d" % (w, n), align_bytes=256)
@@ -76,8 +76,12 @@ def tile_pieceroutedattention_pa_kernel(
             for w in range(2)
         ]
 
-        def load_x(j):
-            nc.sync.dma_start(out=x_sb[j][:], in_=x_tiles_dram[:, j, :])
+        def load_x(first_tile, n_tiles):
+            pair, half = divmod(first_tile, 2)
+            nc.sync.dma_start(
+                out=x_sb[pair][:, half : half + n_tiles, :],
+                in_=x_tiles_dram[:, first_tile : first_tile + n_tiles, :],
+            )
 
         def load_scales(w):
             for quadrant in range(4):
@@ -95,8 +99,10 @@ def tile_pieceroutedattention_pa_kernel(
             )
 
         load_scales(0)
-        for j in range(TOKEN_TILES):
-            load_x(j)
+        for pair in range(PAIRS - 1):
+            load_x(2 * pair, 2)
+        load_x(TOKEN_TILES - 2, 1)
+        load_x(TOKEN_TILES - 1, 1)
         load_words(0, 0, 0, N_SWEEP * PACK)
         load_words(0, 0, N_SWEEP * PACK, N_SWEEP * PACK)
         for w in range(2):
@@ -114,7 +120,7 @@ def tile_pieceroutedattention_pa_kernel(
         ]
 
         def transpose_words(pair, half, g, xt):
-            x_words = x_sb[2 * pair + half][:].bitcast(F32)
+            x_words = x_sb[pair][:, half, :].bitcast(F32)
             for u in range(2):
                 first = WORDS_PER_PASS * g + u
                 nc.tensor.transpose(

@@ -90,12 +90,13 @@ def tile_pieceroutedattention_pa_kernel(
                     in_=weight_scales[w][:, 4 * quadrant : 4 * quadrant + 4, :].bitcast(F32),
                 )
 
-        def load_words(w, n, first_byte, n_bytes):
+        def load_words(w, n, first_byte, n_bytes, first_pass=0, n_passes=PASSES):
             words = weight_words[w].rearrange("g p n t -> p g (n t)")
             start = N_TILE * PACK * n + first_byte
+            passes = slice(first_pass, first_pass + n_passes)
             nc.sync.dma_start(
-                out=w_sb[w][n][:, :, first_byte : first_byte + n_bytes].bitcast(I32),
-                in_=words[:, :, start : start + n_bytes].bitcast(I32),
+                out=w_sb[w][n][:, passes, first_byte : first_byte + n_bytes].bitcast(I32),
+                in_=words[:, passes, start : start + n_bytes].bitcast(I32),
             )
 
         load_scales(0)
@@ -103,7 +104,8 @@ def tile_pieceroutedattention_pa_kernel(
             load_x(2 * pair, 2)
         load_x(TOKEN_TILES - 2, 1)
         load_x(TOKEN_TILES - 1, 1)
-        load_words(0, 0, 0, N_SWEEP * PACK)
+        for g in range(PASSES):
+            load_words(0, 0, 0, N_SWEEP * PACK, g, 1)
         load_words(0, 0, N_SWEEP * PACK, N_SWEEP * PACK)
         for w in range(2):
             for n in range(CHUNKS):
@@ -259,7 +261,8 @@ def tile_pieceroutedattention_pa_kernel(
         last_sweep_pieces = [
             ((0, 1), 0, 2, [(0, 0, 2), (1, 0, 2)]),
             ((2, 3), 0, 2, [(0, 2, 2), (1, 2, 2)]),
-            ((4, 5), 0, 2, [(0, 4, 2), (1, 4, 2)]),
+            ((4,), 0, 2, []),
+            ((5,), 0, 2, [(0, 4, 2), (1, 4, 2)]),
             ((6,), 0, 2, []),
             ((7,), 0, 1, [(0, 6, 2)]),
             ((7,), 1, 1, [(1, 6, 2)]),

@@ -68,13 +68,20 @@ def tile_pieceroutedattention_pa_kernel(
         nc.scalar.activation(out=table_warm[:], in_=eps[:], func=ACT.Abs_reciprocal_sqrt)
 
         x_sb = [keep.tile([P, 2, C], BF16, name="x%d" % i) for i in range(PAIRS)]
-        w_sb = [
-            [
-                keep.tile([P, PASSES, N_TILE * PACK], U8, name="w%d_%d" % (w, n), align_bytes=256)
-                for n in range(CHUNKS)
-            ]
-            for w in range(2)
+        wq_first = keep.tile([P, PASSES, N_TILE * PACK], U8, name="wq_first", align_bytes=256)
+        wq_rest = keep.tile([P, PASSES, 2 * N_TILE * PACK], U8, name="wq_rest", align_bytes=256)
+        wk_sb = [
+            keep.tile([P, HEADS * DH * PACK], U8, name="wk%d" % g, align_bytes=256)
+            for g in range(PASSES)
         ]
+
+        def words_of(w, g, first_byte, n_bytes):
+            if w == 1:
+                return wk_sb[g][:, first_byte : first_byte + n_bytes]
+            chunk = N_TILE * PACK
+            if first_byte < chunk:
+                return wq_first[:, g, first_byte : first_byte + n_bytes]
+            return wq_rest[:, g, first_byte - chunk : first_byte - chunk + n_bytes]
 
         def load_x(first_tile, n_tiles):
             pair, half = divmod(first_tile, 2)
@@ -90,13 +97,12 @@ def tile_pieceroutedattention_pa_kernel(
                     in_=weight_scales[w][:, 4 * quadrant : 4 * quadrant + 4, :].bitcast(F32),
                 )
 
-        def load_words(w, n, first_byte, n_bytes, first_pass=0, n_passes=PASSES):
-            words = weight_words[w].rearrange("g p n t -> p g (n t)")
-            start = N_TILE * PACK * n + first_byte
-            passes = slice(first_pass, first_pass + n_passes)
+        words_dram = [words.rearrange("g p n t -> p g (n t)") for words in weight_words]
+
+        def load_pass(w, g, first_byte, n_bytes):
             nc.sync.dma_start(
-                out=w_sb[w][n][:, passes, first_byte : first_byte + n_bytes].bitcast(I32),
-                in_=words[:, passes, start : start + n_bytes].bitcast(I32),
+                out=words_of(w, g, first_byte, n_bytes).bitcast(I32),
+                in_=words_dram[w][:, g, first_byte : first_byte + n_bytes].bitcast(I32),
             )
 
         load_scales(0)
@@ -104,13 +110,18 @@ def tile_pieceroutedattention_pa_kernel(
             load_x(2 * pair, 2)
         load_x(TOKEN_TILES - 2, 1)
         load_x(TOKEN_TILES - 1, 1)
+        half_chunk = N_SWEEP * PACK
         for g in range(PASSES):
-            load_words(0, 0, 0, N_SWEEP * PACK, g, 1)
-        load_words(0, 0, N_SWEEP * PACK, N_SWEEP * PACK)
-        for w in range(2):
-            for n in range(CHUNKS):
-                if w + n > 0:
-                    load_words(w, n, 0, N_TILE * PACK)
+            load_pass(0, g, 0, half_chunk)
+        nc.sync.dma_start(
+            out=wq_first[:, :, half_chunk:].bitcast(I32),
+            in_=words_dram[0][:, :, half_chunk : 2 * half_chunk].bitcast(I32),
+        )
+        nc.sync.dma_start(
+            out=wq_rest[:].bitcast(I32), in_=words_dram[0][:, :, 2 * half_chunk :].bitcast(I32)
+        )
+        for g in range(PASSES):
+            load_pass(1, g, 0, HEADS * DH * PACK)
 
         x_codes = [
             keep.tile([P, PASSES, 2 * P], U32, name="x_codes%d" % i, align_bytes=256)
@@ -170,11 +181,9 @@ def tile_pieceroutedattention_pa_kernel(
         load_scales(1)
 
         def project(w, base, tiles, first_head, n_heads):
-            n, head_in_chunk = divmod(base + first_head, HEADS_PER_BANK)
             width = DH * n_heads
-            first_word = DH * head_in_chunk
-            word_bytes = slice(PACK * first_word, PACK * (first_word + width))
-            columns = slice(DH * (base + first_head), DH * (base + first_head) + width)
+            first_column = DH * (base + first_head)
+            columns = slice(first_column, first_column + width)
             acc = psum.tile([P, N_TILE], F32, tag="bank")
             for i, j in enumerate(tiles):
                 tokens = slice(P * (j % 2), P * (j % 2 + 1))
@@ -183,7 +192,7 @@ def tile_pieceroutedattention_pa_kernel(
                         out=acc[:, width * i : width * (i + 1)],
                         lhsT=x_codes[j // 2][:, g, tokens].bitcast(FP8X4),
                         lhsT_scale=x_planes[j // 2][:, g, j % 2, 0:P],
-                        rhs=w_sb[w][n][:, g, word_bytes].bitcast(FP8X4),
+                        rhs=words_of(w, g, PACK * first_column, PACK * width).bitcast(FP8X4),
                         rhs_scale=w_planes[w][4 * g : P, columns],
                         start=(g == 0),
                         stop=(g == PASSES - 1),

@@ -59,7 +59,16 @@ def tile_pieceroutedattention_pa_kernel(
         w_planes = [
             keep.tile([P, HEADS * DH], U8, name="w_planes%d" % w, align_bytes=256) for w in range(2)
         ]
-        nc.vector.memset(w_planes[0][:].bitcast(I32), 0)
+        for planes in w_planes:
+            nc.vector.memset(planes[:].bitcast(I32), 0)
+        def load_scales(w, engine):
+            for quadrant in range(4):
+                engine.dma_start(
+                    out=w_planes[w][32 * quadrant : 32 * quadrant + 4 * PASSES, :].bitcast(F32),
+                    in_=weight_scales[w][:, 4 * quadrant : 4 * quadrant + 4, :].bitcast(F32),
+                )
+
+        load_scales(0, nc.scalar)
         eps = keep.tile([P, 1], F32, name="eps")
         nc.vector.memset(eps[:], EPS)
         ident = keep.tile([P, P], F32, name="ident")
@@ -90,13 +99,6 @@ def tile_pieceroutedattention_pa_kernel(
                 in_=x_tiles_dram[:, first_tile : first_tile + n_tiles, :],
             )
 
-        def load_scales(w):
-            for quadrant in range(4):
-                nc.gpsimd.dma_start(
-                    out=w_planes[w][32 * quadrant : 32 * quadrant + 4 * PASSES, :].bitcast(F32),
-                    in_=weight_scales[w][:, 4 * quadrant : 4 * quadrant + 4, :].bitcast(F32),
-                )
-
         words_dram = [words.rearrange("g p n t -> p g (n t)") for words in weight_words]
 
         def load_pass(w, g, first_byte, n_bytes):
@@ -105,7 +107,6 @@ def tile_pieceroutedattention_pa_kernel(
                 in_=words_dram[w][:, g, first_byte : first_byte + n_bytes].bitcast(I32),
             )
 
-        load_scales(0)
         for pair in range(PAIRS - 1):
             load_x(2 * pair, 2)
         load_x(TOKEN_TILES - 2, 1)
@@ -122,6 +123,7 @@ def tile_pieceroutedattention_pa_kernel(
         )
         for g in range(PASSES):
             load_pass(1, g, 0, HEADS * DH * PACK)
+        load_scales(1, nc.sync)
 
         x_codes = [
             keep.tile([P, PASSES, 2 * P], U32, name="x_codes%d" % i, align_bytes=256)
@@ -176,9 +178,6 @@ def tile_pieceroutedattention_pa_kernel(
                     quantise_unit(*copied)
                 copied = (pair, g, grouped)
         quantise_unit(*copied)
-
-        nc.vector.memset(w_planes[1][:].bitcast(I32), 0)
-        load_scales(1)
 
         def project(w, base, tiles, first_head, n_heads):
             width = DH * n_heads

from contextlib import ExitStack

import concourse.masks as masks
import concourse.mybir as mybir

F32 = mybir.dt.float32
BF16 = mybir.dt.bfloat16
I32 = mybir.dt.int32
U32 = mybir.dt.uint32
U8 = mybir.dt.uint8
FP8X4 = mybir.dt.float8_e4m3fn_x4
ACT = mybir.ActivationFunctionType
ALU = mybir.AluOpType

P = 128
PACK = 4
K_PASS = P * PACK
WORDS_PER_PASS = K_PASS // 2

BOARDS, SQUARES, C = 16, 64, 1536
HEADS, DH = 12, 128
TOKENS = BOARDS * SQUARES
TOKEN_TILES = TOKENS // P
PAIRS = TOKEN_TILES // 2
PASSES = C // K_PASS
N_TILE = 512
HEADS_PER_BANK = N_TILE // DH
CHUNKS = HEADS * DH // N_TILE
HEADS_PER_SWEEP = 2
N_SWEEP = HEADS_PER_SWEEP * DH
SWEEPS = HEADS // HEADS_PER_SWEEP
EPS = 2.0 ** -23

FLOPS = 2 * TOKENS * C * 2 * HEADS * DH


def tile_pieceroutedattention_pa_kernel(
    tc, x, Wq_words, Wq_scales, Wk_words, Wk_scales, out_0, out_1
):
    nc = tc.nc
    weight_words = (Wq_words, Wk_words)
    weight_scales = (Wq_scales, Wk_scales)

    x_tiles_dram = x.rearrange("b (s j) c -> (b s) j c", j=TOKEN_TILES)
    out_heads_dram = [
        out.rearrange("b h (s j) d -> h b s (j d)", j=TOKEN_TILES) for out in (out_0, out_1)
    ]

    with ExitStack() as ctx:
        keep = ctx.enter_context(tc.tile_pool(name="keep", bufs=1))
        group_pool = ctx.enter_context(tc.tile_pool(name="group", bufs=4))
        stat_pool = ctx.enter_context(tc.tile_pool(name="stat", bufs=6))
        square_pool = ctx.enter_context(tc.tile_pool(name="square", bufs=2))
        stage_pool = ctx.enter_context(tc.tile_pool(name="stage", bufs=3))
        wide_stage_pool = ctx.enter_context(tc.tile_pool(name="wide_stage", bufs=3))
        psum = ctx.enter_context(tc.psum_pool(name="psum", bufs=8))
        ctx.enter_context(tc.manual_schedule())

        w_planes = [
            keep.tile([P, HEADS * DH], U8, name="w_planes%d" % w, align_bytes=256) for w in range(2)
        ]
        for planes in w_planes:
            nc.vector.memset(planes[:].bitcast(I32), 0)
        def load_scales(w, engine):
            for quadrant in range(4):
                engine.dma_start(
                    out=w_planes[w][32 * quadrant : 32 * quadrant + 4 * PASSES, :].bitcast(F32),
                    in_=weight_scales[w][:, 4 * quadrant : 4 * quadrant + 4, :].bitcast(F32),
                )

        load_scales(0, nc.scalar)
        eps = keep.tile([P, 1], F32, name="eps")
        nc.vector.memset(eps[:], EPS)
        ident = keep.tile([P, P], F32, name="ident")
        masks.make_identity(nc, ident[:])
        table_warm = keep.tile([P, 1], F32, name="table_warm")
        nc.scalar.activation(out=table_warm[:], in_=eps[:], func=ACT.Abs_reciprocal_sqrt)

        x_sb = [keep.tile([P, 2, C], BF16, name="x%d" % i) for i in range(PAIRS)]
        wq_first = keep.tile([P, PASSES, N_TILE * PACK], U8, name="wq_first", align_bytes=256)
        wq_rest = keep.tile([P, PASSES, 2 * N_TILE * PACK], U8, name="wq_rest", align_bytes=256)
        wk_sb = [
            keep.tile([P, HEADS * DH * PACK], U8, name="wk%d" % g, align_bytes=256)
            for g in range(PASSES)
        ]

        def words_of(w, g, first_byte, n_bytes):
            if w == 1:
                return wk_sb[g][:, first_byte : first_byte + n_bytes]
            chunk = N_TILE * PACK
            if first_byte < chunk:
                return wq_first[:, g, first_byte : first_byte + n_bytes]
            return wq_rest[:, g, first_byte - chunk : first_byte - chunk + n_bytes]

        def load_x(first_tile, n_tiles):
            pair, half = divmod(first_tile, 2)
            nc.sync.dma_start(
                out=x_sb[pair][:, half : half + n_tiles, :],
                in_=x_tiles_dram[:, first_tile : first_tile + n_tiles, :],
            )

        words_dram = [words.rearrange("g p n t -> p g (n t)") for words in weight_words]

        def load_pass(w, g, first_byte, n_bytes):
            nc.sync.dma_start(
                out=words_of(w, g, first_byte, n_bytes).bitcast(I32),
                in_=words_dram[w][:, g, first_byte : first_byte + n_bytes].bitcast(I32),
            )

        for pair in range(PAIRS - 1):
            load_x(2 * pair, 2)
        load_x(TOKEN_TILES - 2, 1)
        load_x(TOKEN_TILES - 1, 1)
        half_chunk = N_SWEEP * PACK
        for g in range(PASSES):
            load_pass(0, g, 0, half_chunk)
        nc.sync.dma_start(
            out=wq_first[:, :, half_chunk:].bitcast(I32),
            in_=words_dram[0][:, :, half_chunk : 2 * half_chunk].bitcast(I32),
        )
        nc.sync.dma_start(
            out=wq_rest[:].bitcast(I32), in_=words_dram[0][:, :, 2 * half_chunk :].bitcast(I32)
        )
        for g in range(PASSES):
            load_pass(1, g, 0, HEADS * DH * PACK)
        load_scales(1, nc.sync)

        x_codes = [
            keep.tile([P, PASSES, 2 * P], U32, name="x_codes%d" % i, align_bytes=256)
            for i in range(PAIRS)
        ]
        x_planes = [
            keep.tile([P, PASSES, 2, 2 * P], U8, name="x_planes%d" % i, align_bytes=256)
            for i in range(PAIRS)
        ]

        def transpose_words(pair, half, g, xt):
            x_words = x_sb[pair][:, half, :].bitcast(F32)
            for u in range(2):
                first = WORDS_PER_PASS * g + u
                nc.tensor.transpose(
                    xt[:, half, u, :],
                    x_words[:, first : WORDS_PER_PASS * (g + 1) : 2],
                    ident[:],
                )

        def regroup(g, xt):
            grouped = group_pool.tile([P, 2 * P * PACK], BF16, align_bytes=256)
            grouped_words = grouped[:].bitcast(F32).rearrange(
                "p (half r u) -> p half r u", half=2, u=2
            )
            xt_by_token = xt[:].rearrange("p half u r -> p half r u")
            if g == 0:
                nc.vector.tensor_copy(out=grouped_words, in_=xt_by_token)
            else:
                nc.scalar.copy(out=grouped_words, in_=xt_by_token)
            return grouped

        def quantise_unit(pair, g, grouped):
            for half in range(2):
                nc.vector.quantize_mx(
                    out=x_codes[pair][:, g, P * half : P * (half + 1)].bitcast(FP8X4),
                    scales=x_planes[pair][:, g, half, 0:P],
                    in_=grouped[:, P * PACK * half : P * PACK * (half + 1)],
                )

        copied = None
        for pair in range(PAIRS):
            banks = []
            for g in range(PASSES):
                xt = psum.tile([P, 2, 2, P], F32, tag="bank")
                banks.append(xt)
                transpose_words(pair, 0, g, xt)
            for g in range(PASSES):
                transpose_words(pair, 1, g, banks[g])
                grouped = regroup(g, banks[g])
                if copied is not None:
                    quantise_unit(*copied)
                copied = (pair, g, grouped)
        quantise_unit(*copied)

        def project(w, base, tiles, first_head, n_heads):
            width = DH * n_heads
            first_column = DH * (base + first_head)
            columns = slice(first_column, first_column + width)
            acc = psum.tile([P, N_TILE], F32, tag="bank")
            for i, j in enumerate(tiles):
                tokens = slice(P * (j % 2), P * (j % 2 + 1))
                for g in range(PASSES):
                    nc.tensor.matmul_mx(
                        out=acc[:, width * i : width * (i + 1)],
                        lhsT=x_codes[j // 2][:, g, tokens].bitcast(FP8X4),
                        lhsT_scale=x_planes[j // 2][:, g, j % 2, 0:P],
                        rhs=words_of(w, g, PACK * first_column, PACK * width).bitcast(FP8X4),
                        rhs_scale=w_planes[w][4 * g : P, columns],
                        start=(g == 0),
                        stop=(g == PASSES - 1),
                    )
            return acc

        def sum_squares(acc, squares, sum_sq, first, count):
            for q in range(first, first + count):
                vector = slice(DH * q, DH * (q + 1))
                nc.scalar.activation(
                    out=squares[:, vector],
                    in_=acc[:, vector],
                    func=ACT.Square,
                    accum_out=sum_sq[:, q : q + 1],
                )

        def normalise(acc, sum_sq, tiles, first_head, n_heads, stage):
            count = len(tiles) * n_heads
            rstd = stat_pool.tile([P, N_TILE // DH], F32)
            nc.scalar.activation(
                out=rstd[:, 0:count],
                in_=sum_sq[:, 0:count],
                func=ACT.Abs_reciprocal_sqrt,
                bias=eps[:],
                scale=1.0 / DH,
            )
            nc.vector.tensor_tensor(
                out=stage[
                    :, first_head : first_head + n_heads, tiles[0] : tiles[0] + len(tiles), :
                ].rearrange("p h j d -> p j h d"),
                in0=acc[:, 0 : DH * count].rearrange("p (j h d) -> p j h d", h=n_heads, d=DH),
                in1=rstd[:, 0:count]
                .rearrange("p (j h) -> p j h", h=n_heads)
                .unsqueeze(3)
                .to_broadcast([P, len(tiles), n_heads, DH]),
                op=ALU.mult,
            )

        def store(w, base, head, first_tile, n_tiles, stage):
            nc.sync.dma_start(
                out=out_heads_dram[w][
                    base + head, :, :, DH * first_tile : DH * (first_tile + n_tiles)
                ],
                in_=stage[:, head, first_tile : first_tile + n_tiles, :].rearrange(
                    "p j d -> p (j d)"
                ),
            )

        def finish(w, base, tiles, first_head, n_heads, stores, acc, sum_sq, stage):
            normalise(acc, sum_sq, tiles, first_head, n_heads, stage)
            for head, first_tile, n_tiles in stores:
                store(w, base, head, first_tile, n_tiles, stage)

        sweep_pieces = [
            ((0, 1), 0, 2, []),
            ((2, 3), 0, 2, []),
            ((4, 5), 0, 2, []),
            ((6, 7), 0, 2, [(0, 0, 8), (1, 0, 8)]),
        ]
        wide_pieces = [
            (
                (j,),
                0,
                HEADS_PER_BANK,
                [(h, j - 3, 4) for h in range(HEADS_PER_BANK)] if j % 4 == 3 else [],
            )
            for j in range(TOKEN_TILES)
        ]
        before_last_pieces = [
            ((0, 1), 0, 2, []),
            ((2, 3), 0, 2, [(0, 0, 4), (1, 0, 4)]),
            ((4, 5), 0, 2, []),
            ((6, 7), 0, 2, [(0, 4, 4), (1, 4, 4)]),
        ]
        last_sweep_pieces = [
            ((0, 1), 0, 2, [(0, 0, 2), (1, 0, 2)]),
            ((2, 3), 0, 2, [(0, 2, 2), (1, 2, 2)]),
            ((4,), 0, 2, []),
            ((5,), 0, 2, [(0, 4, 2), (1, 4, 2)]),
            ((6,), 0, 2, []),
            ((7,), 0, 1, [(0, 6, 2)]),
            ((7,), 1, 1, [(1, 6, 2)]),
        ]

        sweeps = [
            (0, 0, sweep_pieces),
            (0, 2, sweep_pieces),
            (0, 4, wide_pieces),
            (0, 8, wide_pieces),
            (1, 0, wide_pieces),
            (1, 4, wide_pieces),
            (1, 8, before_last_pieces),
            (1, 10, last_sweep_pieces),
        ]
        squared = None
        for w, base, pieces in sweeps:
            if pieces[0][2] == HEADS_PER_BANK:
                stage = wide_stage_pool.tile([P, HEADS_PER_BANK, TOKEN_TILES, DH], F32)
            else:
                stage = stage_pool.tile([P, HEADS_PER_SWEEP, TOKEN_TILES, DH], F32)
            for tiles, first_head, n_heads, stores in pieces:
                acc = project(w, base, tiles, first_head, n_heads)
                squares = square_pool.tile([P, N_TILE], F32)
                sum_sq = stat_pool.tile([P, N_TILE // DH], F32)
                sum_squares(acc, squares, sum_sq, 0, 1)
                if squared is not None:
                    finish(*squared)
                sum_squares(acc, squares, sum_sq, 1, len(tiles) * n_heads - 1)
                squared = (w, base, tiles, first_head, n_heads, stores, acc, sum_sq, stage)
        finish(*squared)
